import numpy as np
import ml_dtypes


def mxq(x, axis, fmt="e4m3"):
    dtype, down = {"e4m3": (ml_dtypes.float8_e4m3fn, 7), "e5m2": (ml_dtypes.float8_e5m2, 14)}[fmt]
    v = np.moveaxis(np.asarray(x, np.float32).astype(ml_dtypes.bfloat16).astype(np.float64), axis, -1)
    blocks = v.reshape(v.shape[:-1] + (-1, 32))
    amax = np.abs(blocks).max(-1, keepdims=True)
    byte = np.maximum(np.where(amax > 0, np.frexp(amax)[1] - 1 + 127, 0) - down, 1)
    scale = np.exp2(byte - 127.0)
    codes = (blocks / scale).astype(np.float32).astype(dtype).astype(np.float64)
    return np.moveaxis((codes * scale).reshape(v.shape), -1, axis)


WIDE = False


def mx_kscale(k):
    if not WIDE:
        return np.ones(k)
    levels = np.array([10, -10, 5, -5, 0])
    a = np.random.permutation(np.resize(levels, k // 512 * 4)).reshape(k // 512, 4)
    idx = np.arange(k)
    return np.exp2(a[idx // 512, idx % 128 // 32])


BF16 = ml_dtypes.bfloat16


def bf(x):
    return np.asarray(x, np.float32).astype(BF16)


def f64(x):
    return np.asarray(x).astype(np.float64)


B, S, D_MODEL, N_H, D_H, D_CQ, D_CKV, D_HR = 4, 1024, 1024, 4, 128, 1024, 512, 128
ROPE_BASE = 10000.0


def rope_cos_sin(seq_len, dim):
    inv_freq = 1.0 / (ROPE_BASE ** (np.arange(0, dim, 2) / dim))
    ang = np.arange(seq_len)[:, None] * inv_freq[None, :]
    return np.cos(ang), np.sin(ang)


def rope(t, cos, sin):
    shp = t.shape
    d2 = shp[-1] // 2
    tr = t.reshape(shp[:-1] + (d2, 2))
    x0, x1 = tr[..., 0], tr[..., 1]
    bshape = (1, shp[1]) + (1,) * (x0.ndim - 3) + (d2,)
    cs, sn = cos.reshape(bshape), sin.reshape(bshape)
    return np.stack([x0 * cs - x1 * sn, x0 * sn + x1 * cs], axis=-1).reshape(shp)


def setup_inputs():
    s, t = mx_kscale(D_MODEL), mx_kscale(D_CKV)
    return {"h": bf(np.random.standard_normal((B, S, D_MODEL)) * s),
            "w_ckv": bf(np.random.standard_normal((D_MODEL, D_CKV)) / np.sqrt(D_MODEL) / s[:, None] * t),
            "w_k": bf(np.random.standard_normal((D_CKV, N_H * D_H)) / np.sqrt(D_CKV) / t[:, None]),
            "w_kr": bf(np.random.standard_normal((D_MODEL, D_HR)) / np.sqrt(D_MODEL) / s[:, None]),
            "w_v": bf(np.random.standard_normal((D_CKV, N_H * D_H)) / np.sqrt(D_CKV) / t[:, None])}


def reference(h, w_ckv, w_k, w_kr, w_v):
    cos, sin = rope_cos_sin(S, D_HR)
    hq = mxq(f64(h), 2, "e4m3")
    c_kv = hq @ mxq(f64(w_ckv), 0, "e4m3")
    cq = mxq(c_kv, 2, "e4m3")
    k_c = (cq @ mxq(f64(w_k), 0, "e4m3")).reshape(B, S, N_H, D_H).transpose(0, 2, 1, 3)
    k_r = rope(hq @ mxq(f64(w_kr), 0, "e4m3"), cos, sin)[:, None]
    k = np.concatenate([k_c, np.broadcast_to(k_r, (B, N_H, S, D_HR))], axis=-1)
    v = (cq @ mxq(f64(w_v), 0, "e4m3")).reshape(B, S, N_H, D_H).transpose(0, 2, 1, 3)
    return k, v

@@ -1,0 +1,339 @@
+import math
+from contextlib import ExitStack
+
+import concourse.mybir as mybir
+from concourse.masks import make_identity
+
+F32 = mybir.dt.float32
+BF16 = mybir.dt.bfloat16
+U32 = mybir.dt.uint32
+U8 = mybir.dt.uint8
+I32 = mybir.dt.int32
+FP8X4 = mybir.dt.float8_e4m3fn_x4
+ALU = mybir.AluOpType
+SIN = mybir.ActivationFunctionType.Sin
+
+BATCH, SEQ, D_MODEL, HEADS, D_HEAD, D_LATENT, D_ROPE = 4, 1024, 1024, 4, 128, 512, 128
+ROPE_BASE = 10000.0
+
+P = 128
+PACK = 4
+K_PASS = P * PACK
+H_PASSES = D_MODEL // K_PASS
+SLOTS = SEQ // P
+PAIR = 2
+GROUP = 4
+PAIRS = BATCH * SLOTS // PAIR
+GROUPS = BATCH * SLOTS // GROUP
+ROPE_PAIRS = D_ROPE // 2
+ROUND_MAGIC = 1.5 * 2.0**23
+
+FLOPS = 2 * BATCH * SEQ * (D_MODEL * (D_LATENT + D_ROPE) + 2 * D_LATENT * HEADS * D_HEAD)
+
+
+def tile_mla_pb_t_kernel(tc, h, w_ckv, w_k, w_kr, w_v, out_0, out_1):
+    nc = tc.nc
+    with ExitStack() as stack:
+        stack.enter_context(tc.manual_schedule())
+        consts = stack.enter_context(tc.tile_pool(name="consts", bufs=1))
+        setup = stack.enter_context(tc.tile_pool(name="setup", bufs=1))
+        h_pool = stack.enter_context(tc.tile_pool(name="h_pool", bufs=GROUPS))
+        work = stack.enter_context(tc.tile_pool(name="work", bufs=2))
+        out_pool = stack.enter_context(tc.tile_pool(name="out_pool", bufs=3))
+        xt_psum = stack.enter_context(tc.psum_pool(name="xt_psum", bufs=2))
+        c_psum = stack.enter_context(tc.psum_pool(name="c_psum", bufs=2))
+        u_psum = stack.enter_context(tc.psum_pool(name="u_psum", bufs=1))
+        kv_psum = stack.enter_context(tc.psum_pool(name="kv_psum", bufs=3))
+
+        def h_rows(group):
+            b, first = divmod(group * GROUP, SLOTS)
+            rows = h[b].rearrange("(p t) d -> p (t d)", t=SLOTS)
+            return rows[:, first * D_MODEL : (first + GROUP) * D_MODEL]
+
+        h_tiles = []
+        for group in range(GROUPS):
+            h_sb = h_pool.tile([P, GROUP * D_MODEL], BF16)
+            h_tiles.append(h_sb)
+        half = PAIR * D_MODEL
+        wc_raw = setup.tile([P, H_PASSES, PACK, D_LATENT], BF16)
+        wr_raw = setup.tile([P, H_PASSES, PACK, D_ROPE], BF16)
+        wk_raw = setup.tile([P, PACK, HEADS * D_HEAD], BF16)
+        wv_raw = setup.tile([P, PACK, HEADS * D_HEAD], BF16)
+        for g in range(H_PASSES):
+            nc.sync.dma_start(
+                out=wc_raw[:, g].rearrange("p (u e) c -> p u (e c)", e=2),
+                in_=w_ckv[g * K_PASS : (g + 1) * K_PASS, :].rearrange("(u p e) c -> p u (e c)", p=P, e=2),
+            )
+        nc.sync.dma_start(out=h_tiles[0][:, 0:half], in_=h_rows(0)[:, 0:half])
+        nc.sync.dma_start(
+            out=wr_raw[:].rearrange("p g (u e) c -> p (g u) (e c)", e=2),
+            in_=w_kr.rearrange("(a p e) c -> p a (e c)", p=P, e=2),
+        )
+        nc.sync.dma_start(out=h_tiles[0][:, half:], in_=h_rows(0)[:, half:])
+        nc.sync.dma_start(
+            out=wk_raw[:].rearrange("p j n -> p (j n)"),
+            in_=w_k.rearrange("(p j) n -> p (j n)", j=PACK),
+        )
+        nc.sync.dma_start(
+            out=wv_raw[:].rearrange("p j n -> p (j n)"),
+            in_=w_v.rearrange("(p j) n -> p (j n)", j=PACK),
+        )
+        for group in range(1, GROUPS):
+            nc.sync.dma_start(out=h_tiles[group][:], in_=h_rows(group))
+
+        pos_i = setup.tile([P, SLOTS], I32)
+        nc.gpsimd.iota(pos_i[:], pattern=[[1, SLOTS]], base=0, channel_multiplier=SLOTS)
+        ident = consts.tile([P, P], F32)
+        make_identity(nc, ident[:])
+
+        pos_f = setup.tile([P, SLOTS], F32)
+        nc.vector.tensor_scalar_mul(out=pos_f[:], in0=pos_i[:], scalar1=1.0 / (2.0 * math.pi))
+        freq = setup.tile([P, ROPE_PAIRS], F32)
+        nc.vector.memset(freq[:, 0:1], 1.0)
+        width = 1
+        while width < ROPE_PAIRS:
+            nc.vector.tensor_scalar_mul(
+                out=freq[:, width : 2 * width],
+                in0=freq[:, 0:width],
+                scalar1=ROPE_BASE ** (-2.0 * width / D_ROPE),
+            )
+            width *= 2
+        phase = setup.tile([P, SLOTS, 2, ROPE_PAIRS], F32)
+        nc.vector.tensor_tensor(
+            out=phase[:, :, 1, :],
+            in0=pos_f[:].unsqueeze(2).to_broadcast([P, SLOTS, ROPE_PAIRS]),
+            in1=freq[:].unsqueeze(1).to_broadcast([P, SLOTS, ROPE_PAIRS]),
+            op=ALU.mult,
+        )
+        nc.vector.tensor_scalar_add(out=phase[:, :, 0, :], in0=phase[:, :, 1, :], scalar1=0.25)
+        whole = setup.tile([P, SLOTS, 2, ROPE_PAIRS], F32)
+        nc.vector.tensor_scalar(
+            out=whole[:],
+            in0=phase[:],
+            scalar1=ROUND_MAGIC,
+            scalar2=ROUND_MAGIC,
+            op0=ALU.add,
+            op1=ALU.subtract,
+        )
+        frac = setup.tile([P, SLOTS, 2, ROPE_PAIRS], F32)
+        nc.vector.tensor_sub(out=frac[:], in0=phase[:], in1=whole[:])
+        cos_sin = consts.tile([P, SLOTS, 2, ROPE_PAIRS], F32)
+        nc.scalar.activation(out=cos_sin[:], in_=frac[:], func=SIN, scale=2.0 * math.pi)
+
+        hg_tiles, hq_tiles, cg_tiles, cq_tiles, prod_tiles, out_tiles = {}, {}, {}, {}, {}, {}
+
+        def transpose_h(pair):
+            words = h_tiles[pair // 2][:].bitcast(F32)
+            hg = work.tile([P, PAIR * H_PASSES * P * PACK], BF16, align_bytes=64)
+            hg_tiles[pair] = hg
+            hg_words = hg[:].bitcast(F32).rearrange(
+                "p (i g n u) -> p i g n u", i=PAIR, g=H_PASSES, u=2
+            )
+            for i in range(PAIR):
+                first = ((pair % 2) * PAIR + i) * (D_MODEL // 2)
+                xt = xt_psum.tile([P, 2 * H_PASSES, P], F32)
+                for block in range(2 * H_PASSES):
+                    nc.tensor.transpose(
+                        xt[:, block, :], words[:, first + block * P : first + (block + 1) * P], ident[:]
+                    )
+                nc.scalar.copy(
+                    out=hg_words[:, i], in_=xt[:].rearrange("p (g u) n -> p g n u", u=2)
+                )
+
+        def quantise_h(pair):
+            hq = work.tile([P, PAIR, H_PASSES, P], U32, align_bytes=64)
+            hs = work.tile([P, PAIR, H_PASSES, P], U8, align_bytes=64)
+            hq_tiles[pair] = (hq, hs)
+            nc.vector.quantize_mx(
+                out=hq[:].rearrange("p i g n -> p (i g n)").bitcast(FP8X4),
+                scales=hs[:].rearrange("p i g n -> p (i g n)"),
+                in_=hg_tiles[pair][:],
+            )
+
+        def latent_tile(pair, i):
+            hq, hs = hq_tiles[pair]
+            if i == 0:
+                cg = work.tile([P, PAIR, P, PACK], BF16, align_bytes=64)
+                cg_tiles[pair] = cg
+            c_ps = c_psum.tile([P, PACK, P], F32)
+            for j in range(PACK):
+                for g in range(H_PASSES):
+                    nc.tensor.matmul_mx(
+                        out=c_ps[:, j, :],
+                        lhsT=wc_q[:, g, j, :].bitcast(FP8X4),
+                        lhsT_scale=wc_s[:, g, j, :],
+                        rhs=hq[:, i, g, :].bitcast(FP8X4),
+                        rhs_scale=hs[:, i, g, :],
+                        start=(g == 0),
+                        stop=(g == H_PASSES - 1),
+                    )
+            nc.vector.tensor_copy(
+                out=cg_tiles[pair][:, i], in_=c_ps[:].rearrange("p j n -> p n j")
+            )
+
+        def quantise_latent(pair):
+            cg = cg_tiles[pair]
+            cq = work.tile([P, PAIR, P], U32, align_bytes=64)
+            cs = work.tile([P, PAIR, P], U8, align_bytes=64)
+            cq_tiles[pair] = (cq, cs)
+            nc.vector.quantize_mx(
+                out=cq[:].rearrange("p i n -> p (i n)").bitcast(FP8X4),
+                scales=cs[:].rearrange("p i n -> p (i n)"),
+                in_=cg[:].rearrange("p i n j -> p (i n j)"),
+            )
+
+        def rotary_products(pair):
+            hq, hs = hq_tiles[pair]
+            u_ps = u_psum.tile([P, PAIR, 2, D_ROPE], F32)
+            for i in range(PAIR):
+                for g in range(H_PASSES):
+                    nc.tensor.matmul_mx(
+                        out=u_ps[:, i].rearrange("p c d -> p (c d)"),
+                        lhsT=hq[:, i, g, :].bitcast(FP8X4),
+                        lhsT_scale=hs[:, i, g, :],
+                        rhs=wr_q[:, g, :].bitcast(FP8X4),
+                        rhs_scale=wr_s[:, g, :],
+                        start=(g == 0),
+                        stop=(g == H_PASSES - 1),
+                    )
+            slot = (pair * PAIR) % SLOTS
+            count = PAIR * 2 * ROPE_PAIRS
+            prod = work.tile([P, PAIR, 2, D_ROPE], F32)
+            prod_tiles[pair] = prod
+            nc.vector.tensor_tensor(
+                out=prod[:].rearrange("p i c (r e) -> p (i c r) e", e=2),
+                in0=u_ps[:].rearrange("p i c (r e) -> p (i c r) e", e=2),
+                in1=cos_sin[:, slot : slot + PAIR]
+                .rearrange("p t c r -> p (t c r)")
+                .unsqueeze(2)
+                .to_broadcast([P, count, 2]),
+                op=ALU.mult,
+            )
+
+        def rotary_sum(pair):
+            k_sb = out_tiles[pair // 2][0]
+            prod = prod_tiles[pair]
+            first = (pair % 2) * PAIR
+            nc.vector.tensor_add(
+                out=k_sb[:, 0, first : first + PAIR, D_HEAD:],
+                in0=prod[:, :, 0, :],
+                in1=prod[:, :, 1, :],
+            )
+
+        def rotary_copies(pair):
+            k_sb = out_tiles[pair // 2][0]
+            first = (pair % 2) * PAIR
+            nc.vector.tensor_copy(
+                out=k_sb[:, 1:, first : first + PAIR, D_HEAD:],
+                in_=k_sb[:, 0:1, first : first + PAIR, D_HEAD:].to_broadcast(
+                    [P, HEADS - 1, PAIR, D_ROPE]
+                ),
+            )
+
+        def keys_values_tile(pair, i):
+            cq, cs = cq_tiles[pair]
+            k_sb, v_sb = out_tiles[pair // 2]
+            slot = (pair % 2) * PAIR + i
+            for codes, scales, dst in (
+                (wk_q, wk_s, k_sb[:, :, slot, 0:D_HEAD]),
+                (wv_q, wv_s, v_sb[:, :, slot, :]),
+            ):
+                kv_ps = kv_psum.tile([P, HEADS, D_HEAD], F32)
+                nc.tensor.matmul_mx(
+                    out=kv_ps[:].rearrange("p n d -> p (n d)"),
+                    lhsT=cq[:, i, :].bitcast(FP8X4),
+                    lhsT_scale=cs[:, i, :],
+                    rhs=codes[:].bitcast(FP8X4),
+                    rhs_scale=scales[:],
+                    start=True,
+                    stop=True,
+                )
+                nc.scalar.copy(out=dst, in_=kv_ps[:])
+
+        def store(first_pair, pairs):
+            b, slot = divmod(first_pair * PAIR, SLOTS)
+            first = slot % GROUP
+            tiles = pairs * PAIR
+            for dram, sbuf in zip((out_0, out_1), out_tiles[first_pair // 2]):
+                nc.sync.dma_start(
+                    out=dram[b].rearrange("n (p t) d -> p n t d", t=SLOTS)[:, :, slot : slot + tiles, :],
+                    in_=sbuf[:, :, first : first + tiles, :],
+                )
+
+        def quantise(grouped, codes, scales):
+            nc.vector.quantize_mx(out=codes.bitcast(FP8X4), scales=scales, in_=grouped)
+
+        wc_q = consts.tile([P, H_PASSES, PACK, P], U32, align_bytes=64)
+        wc_s = consts.tile([P, H_PASSES, PACK, P], U8, align_bytes=64)
+        wc_g = setup.tile([P, H_PASSES, PACK, P, PACK], BF16, align_bytes=64)
+        for g in range(H_PASSES):
+            nc.vector.tensor_copy(
+                out=wc_g[:, g], in_=wc_raw[:, g].rearrange("p t (m j) -> p j m t", j=PACK)
+            )
+        transpose_h(0)
+        for g in range(H_PASSES):
+            quantise(
+                wc_g[:, g].rearrange("p j m t -> p (j m t)"),
+                wc_q[:, g].rearrange("p j m -> p (j m)"),
+                wc_s[:, g].rearrange("p j m -> p (j m)"),
+            )
+        quantise_h(0)
+
+        wr_q = consts.tile([P, H_PASSES, 2 * D_ROPE], U32, align_bytes=64)
+        wr_s = consts.tile([P, H_PASSES, 2 * D_ROPE], U8, align_bytes=64)
+        wr_g = setup.tile([P, H_PASSES, 2 * D_ROPE, PACK], BF16, align_bytes=64)
+        nc.vector.tensor_copy(
+            out=wr_g[:, :, 0:D_ROPE, :], in_=wr_raw[:].rearrange("p g t c -> p g c t")
+        )
+        swapped = wr_g[:, :, D_ROPE:, :].rearrange("p g (r e) t -> p g r e t", e=2)
+        plain = wr_raw[:].rearrange("p g t (r e) -> p g r e t", e=2)
+        nc.vector.tensor_scalar_mul(out=swapped[:, :, :, 0, :], in0=plain[:, :, :, 1, :], scalar1=-1.0)
+        nc.vector.tensor_copy(out=swapped[:, :, :, 1, :], in_=plain[:, :, :, 0, :])
+        transpose_h(1)
+        quantise(
+            wr_g[:].rearrange("p g c t -> p (g c t)"),
+            wr_q[:].rearrange("p g c -> p (g c)"),
+            wr_s[:].rearrange("p g c -> p (g c)"),
+        )
+
+        wk_q = consts.tile([P, HEADS * D_HEAD], U32, align_bytes=64)
+        wk_s = consts.tile([P, HEADS * D_HEAD], U8, align_bytes=64)
+        wv_q = consts.tile([P, HEADS * D_HEAD], U32, align_bytes=64)
+        wv_s = consts.tile([P, HEADS * D_HEAD], U8, align_bytes=64)
+        wk_g = setup.tile([P, HEADS * D_HEAD, PACK], BF16, align_bytes=64)
+        wv_g = setup.tile([P, HEADS * D_HEAD, PACK], BF16, align_bytes=64)
+        nc.scalar.copy(out=wk_g[:], in_=wk_raw[:].rearrange("p j n -> p n j"))
+        nc.scalar.copy(out=wv_g[:], in_=wv_raw[:].rearrange("p j n -> p n j"))
+
+        for step in range(PAIRS + 1):
+            entering = step < PAIRS
+            leaving = step >= 1
+            if entering and step % 2 == 0:
+                k_sb = out_pool.tile([P, HEADS, GROUP, D_HEAD + D_ROPE], F32)
+                v_sb = out_pool.tile([P, HEADS, GROUP, D_HEAD], F32)
+                out_tiles[step // 2] = (k_sb, v_sb)
+            if entering:
+                latent_tile(step, 0)
+                rotary_products(step)
+            if leaving:
+                keys_values_tile(step - 1, 0)
+            if step + 1 < PAIRS:
+                quantise_h(step + 1)
+            if entering:
+                latent_tile(step, 1)
+                rotary_sum(step)
+            if leaving:
+                keys_values_tile(step - 1, 1)
+            if entering:
+                quantise_latent(step)
+                rotary_copies(step)
+            if step == 0:
+                quantise(wk_g[:].rearrange("p n j -> p (n j)"), wk_q[:], wk_s[:])
+                quantise(wv_g[:].rearrange("p n j -> p (n j)"), wv_q[:], wv_s[:])
+            if leaving:
+                if (step - 1) // 2 == GROUPS - 1:
+                    store(step - 1, 1)
+                elif (step - 1) % 2 == 1:
+                    store(step - 2, 2)
+            if step + 2 < PAIRS:
+                transpose_h(step + 2)

@@ -117,8 +117,11 @@ def tile_mla_pb_t_kernel(tc, h, w_ckv, w_k, w_kr, w_v, out_0, out_1):
         )
         frac = setup.tile([P, SLOTS, 2, ROPE_PAIRS], F32)
         nc.vector.tensor_sub(out=frac[:], in0=phase[:], in1=whole[:])
-        cos_sin = consts.tile([P, SLOTS, 2, ROPE_PAIRS], F32)
-        nc.scalar.activation(out=cos_sin[:], in_=frac[:], func=SIN, scale=2.0 * math.pi)
+        cos_tab = consts.tile([P, SLOTS, ROPE_PAIRS], F32)
+        sin_tab = consts.tile([P, SLOTS, ROPE_PAIRS, 2], F32)
+        nc.scalar.activation(out=cos_tab[:], in_=frac[:, :, 0, :], func=SIN, scale=2.0 * math.pi)
+        nc.scalar.activation(out=sin_tab[:, :, :, 0], in_=frac[:, :, 1, :], func=SIN, scale=-2.0 * math.pi)
+        nc.scalar.activation(out=sin_tab[:, :, :, 1], in_=frac[:, :, 1, :], func=SIN, scale=2.0 * math.pi)
 
         hg_tiles, hq_tiles, cg_tiles, cq_tiles, prod_tiles, out_tiles = {}, {}, {}, {}, {}, {}
 
@@ -184,11 +187,11 @@ def tile_mla_pb_t_kernel(tc, h, w_ckv, w_k, w_kr, w_v, out_0, out_1):
 
         def rotary_products(pair):
             hq, hs = hq_tiles[pair]
-            u_ps = u_psum.tile([P, PAIR, 2, D_ROPE], F32)
+            u_ps = u_psum.tile([P, PAIR, ROPE_PAIRS, 2], F32)
             for i in range(PAIR):
                 for g in range(H_PASSES):
                     nc.tensor.matmul_mx(
-                        out=u_ps[:, i].rearrange("p c d -> p (c d)"),
+                        out=u_ps[:, i].rearrange("p r e -> p (r e)"),
                         lhsT=hq[:, i, g, :].bitcast(FP8X4),
                         lhsT_scale=hs[:, i, g, :],
                         rhs=wr_q[:, g, :].bitcast(FP8X4),
@@ -197,16 +200,18 @@ def tile_mla_pb_t_kernel(tc, h, w_ckv, w_k, w_kr, w_v, out_0, out_1):
                         stop=(g == H_PASSES - 1),
                     )
             slot = (pair * PAIR) % SLOTS
-            count = PAIR * 2 * ROPE_PAIRS
-            prod = work.tile([P, PAIR, 2, D_ROPE], F32)
+            prod = work.tile([P, 2, PAIR, ROPE_PAIRS, 2], F32)
             prod_tiles[pair] = prod
             nc.vector.tensor_tensor(
-                out=prod[:].rearrange("p i c (r e) -> p (i c r) e", e=2),
-                in0=u_ps[:].rearrange("p i c (r e) -> p (i c r) e", e=2),
-                in1=cos_sin[:, slot : slot + PAIR]
-                .rearrange("p t c r -> p (t c r)")
-                .unsqueeze(2)
-                .to_broadcast([P, count, 2]),
+                out=prod[:, 0],
+                in0=u_ps[:],
+                in1=cos_tab[:, slot : slot + PAIR, :].unsqueeze(3).to_broadcast([P, PAIR, ROPE_PAIRS, 2]),
+                op=ALU.mult,
+            )
+            nc.vector.tensor_tensor(
+                out=prod[:, 1],
+                in0=u_ps[:, :, :, ::-1],
+                in1=sin_tab[:, slot : slot + PAIR],
                 op=ALU.mult,
             )
 
@@ -216,8 +221,8 @@ def tile_mla_pb_t_kernel(tc, h, w_ckv, w_k, w_kr, w_v, out_0, out_1):
             first = (pair % 2) * PAIR
             nc.vector.tensor_add(
                 out=k_sb[:, 0, first : first + PAIR, D_HEAD:],
-                in0=prod[:, :, 0, :],
-                in1=prod[:, :, 1, :],
+                in0=prod[:, 0].rearrange("p i r e -> p i (r e)"),
+                in1=prod[:, 1].rearrange("p i r e -> p i (r e)"),
             )
 
         def rotary_copies(pair):
@@ -279,16 +284,10 @@ def tile_mla_pb_t_kernel(tc, h, w_ckv, w_k, w_kr, w_v, out_0, out_1):
             )
         quantise_h(0)
 
-        wr_q = consts.tile([P, H_PASSES, 2 * D_ROPE], U32, align_bytes=64)
-        wr_s = consts.tile([P, H_PASSES, 2 * D_ROPE], U8, align_bytes=64)
-        wr_g = setup.tile([P, H_PASSES, 2 * D_ROPE, PACK], BF16, align_bytes=64)
-        nc.vector.tensor_copy(
-            out=wr_g[:, :, 0:D_ROPE, :], in_=wr_raw[:].rearrange("p g t c -> p g c t")
-        )
-        swapped = wr_g[:, :, D_ROPE:, :].rearrange("p g (r e) t -> p g r e t", e=2)
-        plain = wr_raw[:].rearrange("p g t (r e) -> p g r e t", e=2)
-        nc.vector.tensor_scalar_mul(out=swapped[:, :, :, 0, :], in0=plain[:, :, :, 1, :], scalar1=-1.0)
-        nc.vector.tensor_copy(out=swapped[:, :, :, 1, :], in_=plain[:, :, :, 0, :])
+        wr_q = consts.tile([P, H_PASSES, D_ROPE], U32, align_bytes=64)
+        wr_s = consts.tile([P, H_PASSES, D_ROPE], U8, align_bytes=64)
+        wr_g = setup.tile([P, H_PASSES, D_ROPE, PACK], BF16, align_bytes=64)
+        nc.vector.tensor_copy(out=wr_g[:], in_=wr_raw[:].rearrange("p g t c -> p g c t"))
         transpose_h(1)
         quantise(
             wr_g[:].rearrange("p g c t -> p (g c t)"),

@@ -255,14 +255,12 @@ def tile_mla_pb_t_kernel(tc, h, w_ckv, w_k, w_kr, w_v, out_0, out_1):
                 )
                 nc.scalar.copy(out=dst, in_=kv_ps[:])
 
-        def store(first_pair, pairs):
-            b, slot = divmod(first_pair * PAIR, SLOTS)
-            first = slot % GROUP
-            tiles = pairs * PAIR
-            for dram, sbuf in zip((out_0, out_1), out_tiles[first_pair // 2]):
+        def store(group):
+            b, slot = divmod(group * GROUP, SLOTS)
+            for dram, sbuf in zip((out_0, out_1), out_tiles[group]):
                 nc.sync.dma_start(
-                    out=dram[b].rearrange("n (p t) d -> p n t d", t=SLOTS)[:, :, slot : slot + tiles, :],
-                    in_=sbuf[:, :, first : first + tiles, :],
+                    out=dram[b].rearrange("n (p t) d -> p n t d", t=SLOTS)[:, :, slot : slot + GROUP, :],
+                    in_=sbuf[:],
                 )
 
         def quantise(grouped, codes, scales):
@@ -329,10 +327,7 @@ def tile_mla_pb_t_kernel(tc, h, w_ckv, w_k, w_kr, w_v, out_0, out_1):
             if step == 0:
                 quantise(wk_g[:].rearrange("p n j -> p (n j)"), wk_q[:], wk_s[:])
                 quantise(wv_g[:].rearrange("p n j -> p (n j)"), wv_q[:], wv_s[:])
-            if leaving:
-                if (step - 1) // 2 == GROUPS - 1:
-                    store(step - 1, 1)
-                elif (step - 1) % 2 == 1:
-                    store(step - 2, 2)
+            if leaving and step % 2 == 0:
+                store((step - 1) // 2)
             if step + 2 < PAIRS:
                 transpose_h(step + 2)

@@ -255,12 +255,13 @@ def tile_mla_pb_t_kernel(tc, h, w_ckv, w_k, w_kr, w_v, out_0, out_1):
                 )
                 nc.scalar.copy(out=dst, in_=kv_ps[:])
 
-        def store(group):
-            b, slot = divmod(group * GROUP, SLOTS)
-            for dram, sbuf in zip((out_0, out_1), out_tiles[group]):
+        def store(pair):
+            b, slot = divmod(pair * PAIR, SLOTS)
+            first = (pair % 2) * PAIR
+            for dram, sbuf in zip((out_0, out_1), out_tiles[pair // 2]):
                 nc.sync.dma_start(
-                    out=dram[b].rearrange("n (p t) d -> p n t d", t=SLOTS)[:, :, slot : slot + GROUP, :],
-                    in_=sbuf[:],
+                    out=dram[b].rearrange("n (p t) d -> p n t d", t=SLOTS)[:, :, slot : slot + PAIR, :],
+                    in_=sbuf[:, :, first : first + PAIR, :],
                 )
 
         def quantise(grouped, codes, scales):
@@ -327,7 +328,7 @@ def tile_mla_pb_t_kernel(tc, h, w_ckv, w_k, w_kr, w_v, out_0, out_1):
             if step == 0:
                 quantise(wk_g[:].rearrange("p n j -> p (n j)"), wk_q[:], wk_s[:])
                 quantise(wv_g[:].rearrange("p n j -> p (n j)"), wv_q[:], wv_s[:])
-            if leaving and step % 2 == 0:
-                store((step - 1) // 2)
+            if leaving:
+                store(step - 1)
             if step + 2 < PAIRS:
                 transpose_h(step + 2)

@@ -86,42 +86,39 @@ def tile_mla_pb_t_kernel(tc, h, w_ckv, w_k, w_kr, w_v, out_0, out_1):
         ident = consts.tile([P, P], F32)
         make_identity(nc, ident[:])
 
-        pos_f = setup.tile([P, SLOTS], F32)
-        nc.vector.tensor_scalar_mul(out=pos_f[:], in0=pos_i[:], scalar1=1.0 / (2.0 * math.pi))
-        freq = setup.tile([P, ROPE_PAIRS], F32)
-        nc.vector.memset(freq[:, 0:1], 1.0)
+        turns = setup.tile([P, SLOTS, ROPE_PAIRS], F32)
+        nc.vector.tensor_scalar_mul(out=turns[:, :, 0], in0=pos_i[:], scalar1=1.0 / (2.0 * math.pi))
         width = 1
         while width < ROPE_PAIRS:
             nc.vector.tensor_scalar_mul(
-                out=freq[:, width : 2 * width],
-                in0=freq[:, 0:width],
+                out=turns[:, :, width : 2 * width],
+                in0=turns[:, :, 0:width],
                 scalar1=ROPE_BASE ** (-2.0 * width / D_ROPE),
             )
             width *= 2
-        phase = setup.tile([P, SLOTS, 2, ROPE_PAIRS], F32)
-        nc.vector.tensor_tensor(
-            out=phase[:, :, 1, :],
-            in0=pos_f[:].unsqueeze(2).to_broadcast([P, SLOTS, ROPE_PAIRS]),
-            in1=freq[:].unsqueeze(1).to_broadcast([P, SLOTS, ROPE_PAIRS]),
-            op=ALU.mult,
-        )
-        nc.vector.tensor_scalar_add(out=phase[:, :, 0, :], in0=phase[:, :, 1, :], scalar1=0.25)
-        whole = setup.tile([P, SLOTS, 2, ROPE_PAIRS], F32)
+        whole = setup.tile([P, SLOTS, ROPE_PAIRS], F32)
         nc.vector.tensor_scalar(
             out=whole[:],
-            in0=phase[:],
+            in0=turns[:],
             scalar1=ROUND_MAGIC,
             scalar2=ROUND_MAGIC,
             op0=ALU.add,
             op1=ALU.subtract,
         )
-        frac = setup.tile([P, SLOTS, 2, ROPE_PAIRS], F32)
-        nc.vector.tensor_sub(out=frac[:], in0=phase[:], in1=whole[:])
+        frac = setup.tile([P, SLOTS, ROPE_PAIRS], F32)
+        nc.vector.tensor_sub(out=frac[:], in0=turns[:], in1=whole[:])
+        quarter = setup.tile([P, SLOTS, ROPE_PAIRS], F32)
+        nc.vector.scalar_tensor_tensor(
+            out=quarter[:], in0=frac[:], scalar=-1.0, in1=frac[:], op0=ALU.mult, op1=ALU.max
+        )
+        nc.vector.tensor_scalar(
+            out=quarter[:], in0=quarter[:], scalar1=-1.0, scalar2=0.25, op0=ALU.mult, op1=ALU.add
+        )
         cos_tab = consts.tile([P, SLOTS, ROPE_PAIRS], F32)
-        sin_tab = consts.tile([P, SLOTS, ROPE_PAIRS, 2], F32)
-        nc.scalar.activation(out=cos_tab[:], in_=frac[:, :, 0, :], func=SIN, scale=2.0 * math.pi)
-        nc.scalar.activation(out=sin_tab[:, :, :, 0], in_=frac[:, :, 1, :], func=SIN, scale=-2.0 * math.pi)
-        nc.scalar.activation(out=sin_tab[:, :, :, 1], in_=frac[:, :, 1, :], func=SIN, scale=2.0 * math.pi)
+        sin_tab = consts.tile([P, SLOTS, 2, ROPE_PAIRS], F32)
+        nc.scalar.activation(out=sin_tab[:, :, 0, :], in_=frac[:], func=SIN, scale=-2.0 * math.pi)
+        nc.scalar.activation(out=sin_tab[:, :, 1, :], in_=frac[:], func=SIN, scale=2.0 * math.pi)
+        nc.scalar.activation(out=cos_tab[:], in_=quarter[:], func=SIN, scale=2.0 * math.pi)
 
         hg_tiles, hq_tiles, cg_tiles, cq_tiles, prod_tiles, out_tiles = {}, {}, {}, {}, {}, {}
 
@@ -187,11 +184,11 @@ def tile_mla_pb_t_kernel(tc, h, w_ckv, w_k, w_kr, w_v, out_0, out_1):
 
         def rotary_products(pair):
             hq, hs = hq_tiles[pair]
-            u_ps = u_psum.tile([P, PAIR, ROPE_PAIRS, 2], F32)
+            u_ps = u_psum.tile([P, PAIR, 2, ROPE_PAIRS], F32)
             for i in range(PAIR):
                 for g in range(H_PASSES):
                     nc.tensor.matmul_mx(
-                        out=u_ps[:, i].rearrange("p r e -> p (r e)"),
+                        out=u_ps[:, i].rearrange("p e r -> p (e r)"),
                         lhsT=hq[:, i, g, :].bitcast(FP8X4),
                         lhsT_scale=hs[:, i, g, :],
                         rhs=wr_q[:, g, :].bitcast(FP8X4),
@@ -200,17 +197,17 @@ def tile_mla_pb_t_kernel(tc, h, w_ckv, w_k, w_kr, w_v, out_0, out_1):
                         stop=(g == H_PASSES - 1),
                     )
             slot = (pair * PAIR) % SLOTS
-            prod = work.tile([P, 2, PAIR, ROPE_PAIRS, 2], F32)
+            prod = work.tile([P, 2, PAIR, 2, ROPE_PAIRS], F32)
             prod_tiles[pair] = prod
             nc.vector.tensor_tensor(
                 out=prod[:, 0],
                 in0=u_ps[:],
-                in1=cos_tab[:, slot : slot + PAIR, :].unsqueeze(3).to_broadcast([P, PAIR, ROPE_PAIRS, 2]),
+                in1=cos_tab[:, slot : slot + PAIR, :].unsqueeze(2).to_broadcast([P, PAIR, 2, ROPE_PAIRS]),
                 op=ALU.mult,
             )
             nc.vector.tensor_tensor(
                 out=prod[:, 1],
-                in0=u_ps[:, :, :, ::-1],
+                in0=u_ps[:, :, ::-1, :],
                 in1=sin_tab[:, slot : slot + PAIR],
                 op=ALU.mult,
             )
@@ -220,9 +217,9 @@ def tile_mla_pb_t_kernel(tc, h, w_ckv, w_k, w_kr, w_v, out_0, out_1):
             prod = prod_tiles[pair]
             first = (pair % 2) * PAIR
             nc.vector.tensor_add(
-                out=k_sb[:, 0, first : first + PAIR, D_HEAD:],
-                in0=prod[:, 0].rearrange("p i r e -> p i (r e)"),
-                in1=prod[:, 1].rearrange("p i r e -> p i (r e)"),
+                out=k_sb[:, 0, first : first + PAIR, D_HEAD:].rearrange("p i (r e) -> p i r e", e=2),
+                in0=prod[:, 0].rearrange("p i e r -> p i r e"),
+                in1=prod[:, 1].rearrange("p i e r -> p i r e"),
             )
 
         def rotary_copies(pair):
@@ -286,7 +283,11 @@ def tile_mla_pb_t_kernel(tc, h, w_ckv, w_k, w_kr, w_v, out_0, out_1):
         wr_q = consts.tile([P, H_PASSES, D_ROPE], U32, align_bytes=64)
         wr_s = consts.tile([P, H_PASSES, D_ROPE], U8, align_bytes=64)
         wr_g = setup.tile([P, H_PASSES, D_ROPE, PACK], BF16, align_bytes=64)
-        nc.vector.tensor_copy(out=wr_g[:], in_=wr_raw[:].rearrange("p g t c -> p g c t"))
+        for g in range(H_PASSES):
+            nc.vector.tensor_copy(
+                out=wr_g[:, g].rearrange("p (e r) t -> p e r t", e=2),
+                in_=wr_raw[:, g].rearrange("p t (r e) -> p e r t", e=2),
+            )
         transpose_h(1)
         quantise(
             wr_g[:].rearrange("p g c t -> p (g c t)"),
@@ -300,8 +301,15 @@ def tile_mla_pb_t_kernel(tc, h, w_ckv, w_k, w_kr, w_v, out_0, out_1):
         wv_s = consts.tile([P, HEADS * D_HEAD], U8, align_bytes=64)
         wk_g = setup.tile([P, HEADS * D_HEAD, PACK], BF16, align_bytes=64)
         wv_g = setup.tile([P, HEADS * D_HEAD, PACK], BF16, align_bytes=64)
-        nc.scalar.copy(out=wk_g[:], in_=wk_raw[:].rearrange("p j n -> p n j"))
-        nc.scalar.copy(out=wv_g[:], in_=wv_raw[:].rearrange("p j n -> p n j"))
+        for grouped, raw in ((wk_g, wk_raw), (wv_g, wv_raw)):
+            nc.gpsimd.tensor_scalar(
+                out=grouped[:],
+                in0=raw[:].rearrange("p j n -> p n j"),
+                scalar1=1.0,
+                scalar2=0.0,
+                op0=ALU.mult,
+                op1=ALU.add,
+            )
 
         for step in range(PAIRS + 1):
             entering = step < PAIRS

@@ -301,15 +301,8 @@ def tile_mla_pb_t_kernel(tc, h, w_ckv, w_k, w_kr, w_v, out_0, out_1):
         wv_s = consts.tile([P, HEADS * D_HEAD], U8, align_bytes=64)
         wk_g = setup.tile([P, HEADS * D_HEAD, PACK], BF16, align_bytes=64)
         wv_g = setup.tile([P, HEADS * D_HEAD, PACK], BF16, align_bytes=64)
-        for grouped, raw in ((wk_g, wk_raw), (wv_g, wv_raw)):
-            nc.gpsimd.tensor_scalar(
-                out=grouped[:],
-                in0=raw[:].rearrange("p j n -> p n j"),
-                scalar1=1.0,
-                scalar2=0.0,
-                op0=ALU.mult,
-                op1=ALU.add,
-            )
+        nc.scalar.copy(out=wk_g[:], in_=wk_raw[:].rearrange("p j n -> p n j"))
+        nc.scalar.copy(out=wv_g[:], in_=wv_raw[:].rearrange("p j n -> p n j"))
 
         for step in range(PAIRS + 1):
             entering = step < PAIRS

@@ -115,9 +115,8 @@ def tile_mla_pb_t_kernel(tc, h, w_ckv, w_k, w_kr, w_v, out_0, out_1):
             out=quarter[:], in0=quarter[:], scalar1=-1.0, scalar2=0.25, op0=ALU.mult, op1=ALU.add
         )
         cos_tab = consts.tile([P, SLOTS, ROPE_PAIRS], F32)
-        sin_tab = consts.tile([P, SLOTS, 2, ROPE_PAIRS], F32)
-        nc.scalar.activation(out=sin_tab[:, :, 0, :], in_=frac[:], func=SIN, scale=-2.0 * math.pi)
-        nc.scalar.activation(out=sin_tab[:, :, 1, :], in_=frac[:], func=SIN, scale=2.0 * math.pi)
+        sin_tab = consts.tile([P, SLOTS, ROPE_PAIRS, 2], F32)
+        nc.scalar.activation(out=sin_tab[:, :, :, 0], in_=frac[:], func=SIN, scale=-2.0 * math.pi)
         nc.scalar.activation(out=cos_tab[:], in_=quarter[:], func=SIN, scale=2.0 * math.pi)
 
         hg_tiles, hq_tiles, cg_tiles, cq_tiles, prod_tiles, out_tiles = {}, {}, {}, {}, {}, {}
@@ -184,11 +183,11 @@ def tile_mla_pb_t_kernel(tc, h, w_ckv, w_k, w_kr, w_v, out_0, out_1):
 
         def rotary_products(pair):
             hq, hs = hq_tiles[pair]
-            u_ps = u_psum.tile([P, PAIR, 2, ROPE_PAIRS], F32)
+            u_ps = u_psum.tile([P, PAIR, ROPE_PAIRS, 2], F32)
             for i in range(PAIR):
                 for g in range(H_PASSES):
                     nc.tensor.matmul_mx(
-                        out=u_ps[:, i].rearrange("p e r -> p (e r)"),
+                        out=u_ps[:, i].rearrange("p r e -> p (r e)"),
                         lhsT=hq[:, i, g, :].bitcast(FP8X4),
                         lhsT_scale=hs[:, i, g, :],
                         rhs=wr_q[:, g, :].bitcast(FP8X4),
@@ -197,17 +196,17 @@ def tile_mla_pb_t_kernel(tc, h, w_ckv, w_k, w_kr, w_v, out_0, out_1):
                         stop=(g == H_PASSES - 1),
                     )
             slot = (pair * PAIR) % SLOTS
-            prod = work.tile([P, 2, PAIR, 2, ROPE_PAIRS], F32)
+            prod = work.tile([P, 2, PAIR, ROPE_PAIRS, 2], F32)
             prod_tiles[pair] = prod
             nc.vector.tensor_tensor(
                 out=prod[:, 0],
                 in0=u_ps[:],
-                in1=cos_tab[:, slot : slot + PAIR, :].unsqueeze(2).to_broadcast([P, PAIR, 2, ROPE_PAIRS]),
+                in1=cos_tab[:, slot : slot + PAIR, :].unsqueeze(3).to_broadcast([P, PAIR, ROPE_PAIRS, 2]),
                 op=ALU.mult,
             )
             nc.vector.tensor_tensor(
                 out=prod[:, 1],
-                in0=u_ps[:, :, ::-1, :],
+                in0=u_ps[:, :, :, ::-1],
                 in1=sin_tab[:, slot : slot + PAIR],
                 op=ALU.mult,
             )
@@ -217,9 +216,9 @@ def tile_mla_pb_t_kernel(tc, h, w_ckv, w_k, w_kr, w_v, out_0, out_1):
             prod = prod_tiles[pair]
             first = (pair % 2) * PAIR
             nc.vector.tensor_add(
-                out=k_sb[:, 0, first : first + PAIR, D_HEAD:].rearrange("p i (r e) -> p i r e", e=2),
-                in0=prod[:, 0].rearrange("p i e r -> p i r e"),
-                in1=prod[:, 1].rearrange("p i e r -> p i r e"),
+                out=k_sb[:, 0, first : first + PAIR, D_HEAD:],
+                in0=prod[:, 0].rearrange("p i r e -> p i (r e)"),
+                in1=prod[:, 1].rearrange("p i r e -> p i (r e)"),
             )
 
         def rotary_copies(pair):
@@ -272,6 +271,7 @@ def tile_mla_pb_t_kernel(tc, h, w_ckv, w_k, w_kr, w_v, out_0, out_1):
                 out=wc_g[:, g], in_=wc_raw[:, g].rearrange("p t (m j) -> p j m t", j=PACK)
             )
         transpose_h(0)
+        nc.scalar.activation(out=sin_tab[:, :, :, 1], in_=frac[:], func=SIN, scale=2.0 * math.pi)
         for g in range(H_PASSES):
             quantise(
                 wc_g[:, g].rearrange("p j m t -> p (j m t)"),
@@ -283,11 +283,7 @@ def tile_mla_pb_t_kernel(tc, h, w_ckv, w_k, w_kr, w_v, out_0, out_1):
         wr_q = consts.tile([P, H_PASSES, D_ROPE], U32, align_bytes=64)
         wr_s = consts.tile([P, H_PASSES, D_ROPE], U8, align_bytes=64)
         wr_g = setup.tile([P, H_PASSES, D_ROPE, PACK], BF16, align_bytes=64)
-        for g in range(H_PASSES):
-            nc.vector.tensor_copy(
-                out=wr_g[:, g].rearrange("p (e r) t -> p e r t", e=2),
-                in_=wr_raw[:, g].rearrange("p t (r e) -> p e r t", e=2),
-            )
+        nc.vector.tensor_copy(out=wr_g[:], in_=wr_raw[:].rearrange("p g t c -> p g c t"))
         transpose_h(1)
         quantise(
             wr_g[:].rearrange("p g c t -> p (g c t)"),

@@ -21,6 +21,7 @@ PACK = 4
 K_PASS = P * PACK
 H_PASSES = D_MODEL // K_PASS
 SLOTS = SEQ // P
+LINE = 256
 PAIR = 2
 GROUP = 4
 PAIRS = BATCH * SLOTS // PAIR
@@ -52,13 +53,13 @@ def tile_mla_pb_t_kernel(tc, h, w_ckv, w_k, w_kr, w_v, out_0, out_1):
 
         h_tiles = []
         for group in range(GROUPS):
-            h_sb = h_pool.tile([P, GROUP * D_MODEL], BF16)
+            h_sb = h_pool.tile([P, GROUP * D_MODEL], BF16, align_bytes=LINE)
             h_tiles.append(h_sb)
         half = PAIR * D_MODEL
-        wc_raw = setup.tile([P, H_PASSES, PACK, D_LATENT], BF16)
-        wr_raw = setup.tile([P, H_PASSES, PACK, D_ROPE], BF16)
-        wk_raw = setup.tile([P, PACK, HEADS * D_HEAD], BF16)
-        wv_raw = setup.tile([P, PACK, HEADS * D_HEAD], BF16)
+        wc_raw = setup.tile([P, H_PASSES, PACK, D_LATENT], BF16, align_bytes=LINE)
+        wr_raw = setup.tile([P, H_PASSES, PACK, D_ROPE], BF16, align_bytes=LINE)
+        wk_raw = setup.tile([P, PACK, HEADS * D_HEAD], BF16, align_bytes=LINE)
+        wv_raw = setup.tile([P, PACK, HEADS * D_HEAD], BF16, align_bytes=LINE)
         for g in range(H_PASSES):
             nc.sync.dma_start(
                 out=wc_raw[:, g].rearrange("p (u e) c -> p u (e c)", e=2),
@@ -81,12 +82,12 @@ def tile_mla_pb_t_kernel(tc, h, w_ckv, w_k, w_kr, w_v, out_0, out_1):
         for group in range(1, GROUPS):
             nc.sync.dma_start(out=h_tiles[group][:], in_=h_rows(group))
 
-        pos_i = setup.tile([P, SLOTS], I32)
+        pos_i = setup.tile([P, SLOTS], I32, align_bytes=LINE)
         nc.gpsimd.iota(pos_i[:], pattern=[[1, SLOTS]], base=0, channel_multiplier=SLOTS)
-        ident = consts.tile([P, P], F32)
+        ident = consts.tile([P, P], F32, align_bytes=LINE)
         make_identity(nc, ident[:])
 
-        turns = setup.tile([P, SLOTS, ROPE_PAIRS], F32)
+        turns = setup.tile([P, SLOTS, ROPE_PAIRS], F32, align_bytes=LINE)
         nc.vector.tensor_scalar_mul(out=turns[:, :, 0], in0=pos_i[:], scalar1=1.0 / (2.0 * math.pi))
         width = 1
         while width < ROPE_PAIRS:
@@ -96,7 +97,7 @@ def tile_mla_pb_t_kernel(tc, h, w_ckv, w_k, w_kr, w_v, out_0, out_1):
                 scalar1=ROPE_BASE ** (-2.0 * width / D_ROPE),
             )
             width *= 2
-        whole = setup.tile([P, SLOTS, ROPE_PAIRS], F32)
+        whole = setup.tile([P, SLOTS, ROPE_PAIRS], F32, align_bytes=LINE)
         nc.vector.tensor_scalar(
             out=whole[:],
             in0=turns[:],
@@ -105,17 +106,17 @@ def tile_mla_pb_t_kernel(tc, h, w_ckv, w_k, w_kr, w_v, out_0, out_1):
             op0=ALU.add,
             op1=ALU.subtract,
         )
-        frac = setup.tile([P, SLOTS, ROPE_PAIRS], F32)
+        frac = setup.tile([P, SLOTS, ROPE_PAIRS], F32, align_bytes=LINE)
         nc.vector.tensor_sub(out=frac[:], in0=turns[:], in1=whole[:])
-        quarter = setup.tile([P, SLOTS, ROPE_PAIRS], F32)
+        quarter = setup.tile([P, SLOTS, ROPE_PAIRS], F32, align_bytes=LINE)
         nc.vector.scalar_tensor_tensor(
             out=quarter[:], in0=frac[:], scalar=-1.0, in1=frac[:], op0=ALU.mult, op1=ALU.max
         )
         nc.vector.tensor_scalar(
             out=quarter[:], in0=quarter[:], scalar1=-1.0, scalar2=0.25, op0=ALU.mult, op1=ALU.add
         )
-        cos_tab = consts.tile([P, SLOTS, ROPE_PAIRS], F32)
-        sin_tab = consts.tile([P, SLOTS, ROPE_PAIRS, 2], F32)
+        cos_tab = consts.tile([P, SLOTS, ROPE_PAIRS], F32, align_bytes=LINE)
+        sin_tab = consts.tile([P, SLOTS, ROPE_PAIRS, 2], F32, align_bytes=LINE)
         nc.scalar.activation(out=sin_tab[:, :, :, 0], in_=frac[:], func=SIN, scale=-2.0 * math.pi)
         nc.scalar.activation(out=cos_tab[:], in_=quarter[:], func=SIN, scale=2.0 * math.pi)
 
@@ -123,7 +124,7 @@ def tile_mla_pb_t_kernel(tc, h, w_ckv, w_k, w_kr, w_v, out_0, out_1):
 
         def transpose_h(pair):
             words = h_tiles[pair // 2][:].bitcast(F32)
-            hg = work.tile([P, PAIR * H_PASSES * P * PACK], BF16, align_bytes=64)
+            hg = work.tile([P, PAIR * H_PASSES * P * PACK], BF16, align_bytes=LINE)
             hg_tiles[pair] = hg
             hg_words = hg[:].bitcast(F32).rearrange(
                 "p (i g n u) -> p i g n u", i=PAIR, g=H_PASSES, u=2
@@ -140,8 +141,8 @@ def tile_mla_pb_t_kernel(tc, h, w_ckv, w_k, w_kr, w_v, out_0, out_1):
                 )
 
         def quantise_h(pair):
-            hq = work.tile([P, PAIR, H_PASSES, P], U32, align_bytes=64)
-            hs = work.tile([P, PAIR, H_PASSES, P], U8, align_bytes=64)
+            hq = work.tile([P, PAIR, H_PASSES, P], U32, align_bytes=LINE)
+            hs = work.tile([P, PAIR, H_PASSES, P], U8, align_bytes=LINE)
             hq_tiles[pair] = (hq, hs)
             nc.vector.quantize_mx(
                 out=hq[:].rearrange("p i g n -> p (i g n)").bitcast(FP8X4),
@@ -152,7 +153,7 @@ def tile_mla_pb_t_kernel(tc, h, w_ckv, w_k, w_kr, w_v, out_0, out_1):
         def latent_tile(pair, i):
             hq, hs = hq_tiles[pair]
             if i == 0:
-                cg = work.tile([P, PAIR, P, PACK], BF16, align_bytes=64)
+                cg = work.tile([P, PAIR, P, PACK], BF16, align_bytes=LINE)
                 cg_tiles[pair] = cg
             c_ps = c_psum.tile([P, PACK, P], F32)
             for j in range(PACK):
@@ -172,8 +173,8 @@ def tile_mla_pb_t_kernel(tc, h, w_ckv, w_k, w_kr, w_v, out_0, out_1):
 
         def quantise_latent(pair):
             cg = cg_tiles[pair]
-            cq = work.tile([P, PAIR, P], U32, align_bytes=64)
-            cs = work.tile([P, PAIR, P], U8, align_bytes=64)
+            cq = work.tile([P, PAIR, P], U32, align_bytes=LINE)
+            cs = work.tile([P, PAIR, P], U8, align_bytes=LINE)
             cq_tiles[pair] = (cq, cs)
             nc.vector.quantize_mx(
                 out=cq[:].rearrange("p i n -> p (i n)").bitcast(FP8X4),
@@ -196,7 +197,7 @@ def tile_mla_pb_t_kernel(tc, h, w_ckv, w_k, w_kr, w_v, out_0, out_1):
                         stop=(g == H_PASSES - 1),
                     )
             slot = (pair * PAIR) % SLOTS
-            prod = work.tile([P, 2, PAIR, ROPE_PAIRS, 2], F32)
+            prod = work.tile([P, 2, PAIR, ROPE_PAIRS, 2], F32, align_bytes=LINE)
             prod_tiles[pair] = prod
             nc.vector.tensor_tensor(
                 out=prod[:, 0],
@@ -263,9 +264,9 @@ def tile_mla_pb_t_kernel(tc, h, w_ckv, w_k, w_kr, w_v, out_0, out_1):
         def quantise(grouped, codes, scales):
             nc.vector.quantize_mx(out=codes.bitcast(FP8X4), scales=scales, in_=grouped)
 
-        wc_q = consts.tile([P, H_PASSES, PACK, P], U32, align_bytes=64)
-        wc_s = consts.tile([P, H_PASSES, PACK, P], U8, align_bytes=64)
-        wc_g = setup.tile([P, H_PASSES, PACK, P, PACK], BF16, align_bytes=64)
+        wc_q = consts.tile([P, H_PASSES, PACK, P], U32, align_bytes=LINE)
+        wc_s = consts.tile([P, H_PASSES, PACK, P], U8, align_bytes=LINE)
+        wc_g = setup.tile([P, H_PASSES, PACK, P, PACK], BF16, align_bytes=LINE)
         for g in range(H_PASSES):
             nc.vector.tensor_copy(
                 out=wc_g[:, g], in_=wc_raw[:, g].rearrange("p t (m j) -> p j m t", j=PACK)
@@ -280,9 +281,9 @@ def tile_mla_pb_t_kernel(tc, h, w_ckv, w_k, w_kr, w_v, out_0, out_1):
             )
         quantise_h(0)
 
-        wr_q = consts.tile([P, H_PASSES, D_ROPE], U32, align_bytes=64)
-        wr_s = consts.tile([P, H_PASSES, D_ROPE], U8, align_bytes=64)
-        wr_g = setup.tile([P, H_PASSES, D_ROPE, PACK], BF16, align_bytes=64)
+        wr_q = consts.tile([P, H_PASSES, D_ROPE], U32, align_bytes=LINE)
+        wr_s = consts.tile([P, H_PASSES, D_ROPE], U8, align_bytes=LINE)
+        wr_g = setup.tile([P, H_PASSES, D_ROPE, PACK], BF16, align_bytes=LINE)
         nc.vector.tensor_copy(out=wr_g[:], in_=wr_raw[:].rearrange("p g t c -> p g c t"))
         transpose_h(1)
         quantise(
@@ -291,12 +292,12 @@ def tile_mla_pb_t_kernel(tc, h, w_ckv, w_k, w_kr, w_v, out_0, out_1):
             wr_s[:].rearrange("p g c -> p (g c)"),
         )
 
-        wk_q = consts.tile([P, HEADS * D_HEAD], U32, align_bytes=64)
-        wk_s = consts.tile([P, HEADS * D_HEAD], U8, align_bytes=64)
-        wv_q = consts.tile([P, HEADS * D_HEAD], U32, align_bytes=64)
-        wv_s = consts.tile([P, HEADS * D_HEAD], U8, align_bytes=64)
-        wk_g = setup.tile([P, HEADS * D_HEAD, PACK], BF16, align_bytes=64)
-        wv_g = setup.tile([P, HEADS * D_HEAD, PACK], BF16, align_bytes=64)
+        wk_q = consts.tile([P, HEADS * D_HEAD], U32, align_bytes=LINE)
+        wk_s = consts.tile([P, HEADS * D_HEAD], U8, align_bytes=LINE)
+        wv_q = consts.tile([P, HEADS * D_HEAD], U32, align_bytes=LINE)
+        wv_s = consts.tile([P, HEADS * D_HEAD], U8, align_bytes=LINE)
+        wk_g = setup.tile([P, HEADS * D_HEAD, PACK], BF16, align_bytes=LINE)
+        wv_g = setup.tile([P, HEADS * D_HEAD, PACK], BF16, align_bytes=LINE)
         nc.scalar.copy(out=wk_g[:], in_=wk_raw[:].rearrange("p j n -> p n j"))
         nc.scalar.copy(out=wv_g[:], in_=wv_raw[:].rearrange("p j n -> p n j"))
 
@@ -304,8 +305,8 @@ def tile_mla_pb_t_kernel(tc, h, w_ckv, w_k, w_kr, w_v, out_0, out_1):
             entering = step < PAIRS
             leaving = step >= 1
             if entering and step % 2 == 0:
-                k_sb = out_pool.tile([P, HEADS, GROUP, D_HEAD + D_ROPE], F32)
-                v_sb = out_pool.tile([P, HEADS, GROUP, D_HEAD], F32)
+                k_sb = out_pool.tile([P, HEADS, GROUP, D_HEAD + D_ROPE], F32, align_bytes=LINE)
+                v_sb = out_pool.tile([P, HEADS, GROUP, D_HEAD], F32, align_bytes=LINE)
                 out_tiles[step // 2] = (k_sb, v_sb)
             if entering:
                 latent_tile(step, 0)

@@ -38,7 +38,7 @@ def tile_mla_pb_t_kernel(tc, h, w_ckv, w_k, w_kr, w_v, out_0, out_1):
         stack.enter_context(tc.manual_schedule())
         consts = stack.enter_context(tc.tile_pool(name="consts", bufs=1))
         setup = stack.enter_context(tc.tile_pool(name="setup", bufs=1))
-        h_pool = stack.enter_context(tc.tile_pool(name="h_pool", bufs=GROUPS))
+        h_pool = stack.enter_context(tc.tile_pool(name="h_pool", bufs=1))
         work = stack.enter_context(tc.tile_pool(name="work", bufs=2))
         out_pool = stack.enter_context(tc.tile_pool(name="out_pool", bufs=3))
         xt_psum = stack.enter_context(tc.psum_pool(name="xt_psum", bufs=2))
@@ -46,16 +46,13 @@ def tile_mla_pb_t_kernel(tc, h, w_ckv, w_k, w_kr, w_v, out_0, out_1):
         u_psum = stack.enter_context(tc.psum_pool(name="u_psum", bufs=1))
         kv_psum = stack.enter_context(tc.psum_pool(name="kv_psum", bufs=3))
 
-        def h_rows(group):
-            b, first = divmod(group * GROUP, SLOTS)
-            rows = h[b].rearrange("(p t) d -> p (t d)", t=SLOTS)
-            return rows[:, first * D_MODEL : (first + GROUP) * D_MODEL]
+        h_sb = h_pool.tile([P, BATCH, SLOTS * D_MODEL], BF16, align_bytes=LINE)
+        h_rows = h.rearrange("b (p t) d -> p b (t d)", t=SLOTS)
 
-        h_tiles = []
-        for group in range(GROUPS):
-            h_sb = h_pool.tile([P, GROUP * D_MODEL], BF16, align_bytes=LINE)
-            h_tiles.append(h_sb)
-        half = PAIR * D_MODEL
+        def load_h(batches, tiles):
+            rows = slice(tiles.start * D_MODEL, tiles.stop * D_MODEL)
+            nc.sync.dma_start(out=h_sb[:, batches, rows], in_=h_rows[:, batches, rows])
+
         wc_raw = setup.tile([P, H_PASSES, PACK, D_LATENT], BF16, align_bytes=LINE)
         wr_raw = setup.tile([P, H_PASSES, PACK, D_ROPE], BF16, align_bytes=LINE)
         wk_raw = setup.tile([P, PACK, HEADS * D_HEAD], BF16, align_bytes=LINE)
@@ -65,12 +62,12 @@ def tile_mla_pb_t_kernel(tc, h, w_ckv, w_k, w_kr, w_v, out_0, out_1):
                 out=wc_raw[:, g].rearrange("p (u e) c -> p u (e c)", e=2),
                 in_=w_ckv[g * K_PASS : (g + 1) * K_PASS, :].rearrange("(u p e) c -> p u (e c)", p=P, e=2),
             )
-        nc.sync.dma_start(out=h_tiles[0][:, 0:half], in_=h_rows(0)[:, 0:half])
+        load_h(slice(0, 1), slice(0, PAIR))
         nc.sync.dma_start(
             out=wr_raw[:].rearrange("p g (u e) c -> p (g u) (e c)", e=2),
             in_=w_kr.rearrange("(a p e) c -> p a (e c)", p=P, e=2),
         )
-        nc.sync.dma_start(out=h_tiles[0][:, half:], in_=h_rows(0)[:, half:])
+        load_h(slice(0, 1), slice(PAIR, GROUP))
         nc.sync.dma_start(
             out=wk_raw[:].rearrange("p j n -> p (j n)"),
             in_=w_k.rearrange("(p j) n -> p (j n)", j=PACK),
@@ -79,8 +76,9 @@ def tile_mla_pb_t_kernel(tc, h, w_ckv, w_k, w_kr, w_v, out_0, out_1):
             out=wv_raw[:].rearrange("p j n -> p (j n)"),
             in_=w_v.rearrange("(p j) n -> p (j n)", j=PACK),
         )
-        for group in range(1, GROUPS):
-            nc.sync.dma_start(out=h_tiles[group][:], in_=h_rows(group))
+        load_h(slice(0, 1), slice(GROUP, SLOTS))
+        load_h(slice(1, 2), slice(0, SLOTS))
+        load_h(slice(2, BATCH), slice(0, SLOTS))
 
         pos_i = setup.tile([P, SLOTS], I32, align_bytes=LINE)
         nc.gpsimd.iota(pos_i[:], pattern=[[1, SLOTS]], base=0, channel_multiplier=SLOTS)
@@ -123,14 +121,15 @@ def tile_mla_pb_t_kernel(tc, h, w_ckv, w_k, w_kr, w_v, out_0, out_1):
         hg_tiles, hq_tiles, cg_tiles, cq_tiles, prod_tiles, out_tiles = {}, {}, {}, {}, {}, {}
 
         def transpose_h(pair):
-            words = h_tiles[pair // 2][:].bitcast(F32)
+            b, slot = divmod(pair * PAIR, SLOTS)
+            words = h_sb[:, b].bitcast(F32)
             hg = work.tile([P, PAIR * H_PASSES * P * PACK], BF16, align_bytes=LINE)
             hg_tiles[pair] = hg
             hg_words = hg[:].bitcast(F32).rearrange(
                 "p (i g n u) -> p i g n u", i=PAIR, g=H_PASSES, u=2
             )
             for i in range(PAIR):
-                first = ((pair % 2) * PAIR + i) * (D_MODEL // 2)
+                first = (slot + i) * (D_MODEL // 2)
                 xt = xt_psum.tile([P, 2 * H_PASSES, P], F32)
                 for block in range(2 * H_PASSES):
                     nc.tensor.transpose(
@@ -236,9 +235,10 @@ def tile_mla_pb_t_kernel(tc, h, w_ckv, w_k, w_kr, w_v, out_0, out_1):
             cq, cs = cq_tiles[pair]
             k_sb, v_sb = out_tiles[pair // 2]
             slot = (pair % 2) * PAIR + i
-            for codes, scales, dst in (
-                (wk_q, wk_s, k_sb[:, :, slot, 0:D_HEAD]),
-                (wv_q, wv_s, v_sb[:, :, slot, :]),
+            v_copy = nc.vector.tensor_copy if pair == PAIRS - 1 else nc.scalar.copy
+            for codes, scales, dst, copy in (
+                (wk_q, wk_s, k_sb[:, :, slot, 0:D_HEAD], nc.scalar.copy),
+                (wv_q, wv_s, v_sb[:, :, slot, :], v_copy),
             ):
                 kv_ps = kv_psum.tile([P, HEADS, D_HEAD], F32)
                 nc.tensor.matmul_mx(
@@ -250,16 +250,27 @@ def tile_mla_pb_t_kernel(tc, h, w_ckv, w_k, w_kr, w_v, out_0, out_1):
                     start=True,
                     stop=True,
                 )
-                nc.scalar.copy(out=dst, in_=kv_ps[:])
+                copy(out=dst, in_=kv_ps[:])
 
-        def store(pair):
-            b, slot = divmod(pair * PAIR, SLOTS)
-            first = (pair % 2) * PAIR
-            for dram, sbuf in zip((out_0, out_1), out_tiles[pair // 2]):
-                nc.sync.dma_start(
-                    out=dram[b].rearrange("n (p t) d -> p n t d", t=SLOTS)[:, :, slot : slot + PAIR, :],
-                    in_=sbuf[:, :, first : first + PAIR, :],
-                )
+        def store(dram, sbuf, group, first, count):
+            b, slot = divmod(group * GROUP + first, SLOTS)
+            nc.sync.dma_start(
+                out=dram[b].rearrange("n (p t) d -> p n t d", t=SLOTS)[:, :, slot : slot + count, :],
+                in_=sbuf[:, :, first : first + count, :],
+            )
+
+        def store_pair(pair):
+            group, odd = divmod(pair, 2)
+            k_sb, v_sb = out_tiles[group]
+            store(out_0, k_sb, group, odd * PAIR, PAIR)
+            if group in (0, GROUPS - 1):
+                store(out_1, v_sb, group, odd * PAIR, PAIR)
+            elif odd:
+                store(out_1, v_sb, group, 0, GROUP)
+
+        def store_last_tile(i):
+            for dram, sbuf in zip((out_0, out_1), out_tiles[GROUPS - 1]):
+                store(dram, sbuf, GROUPS - 1, GROUP - PAIR + i, 1)
 
         def quantise(grouped, codes, scales):
             nc.vector.quantize_mx(out=codes.bitcast(FP8X4), scales=scales, in_=grouped)
@@ -313,6 +324,8 @@ def tile_mla_pb_t_kernel(tc, h, w_ckv, w_k, w_kr, w_v, out_0, out_1):
                 rotary_products(step)
             if leaving:
                 keys_values_tile(step - 1, 0)
+                if step == PAIRS:
+                    store_last_tile(0)
             if step + 1 < PAIRS:
                 quantise_h(step + 1)
             if entering:
@@ -320,13 +333,15 @@ def tile_mla_pb_t_kernel(tc, h, w_ckv, w_k, w_kr, w_v, out_0, out_1):
                 rotary_sum(step)
             if leaving:
                 keys_values_tile(step - 1, 1)
+                if step == PAIRS:
+                    store_last_tile(1)
             if entering:
                 quantise_latent(step)
                 rotary_copies(step)
             if step == 0:
                 quantise(wk_g[:].rearrange("p n j -> p (n j)"), wk_q[:], wk_s[:])
                 quantise(wv_g[:].rearrange("p n j -> p (n j)"), wv_q[:], wv_s[:])
-            if leaving:
-                store(step - 1)
+            if leaving and step < PAIRS:
+                store_pair(step - 1)
             if step + 2 < PAIRS:
                 transpose_h(step + 2)

import math
from contextlib import ExitStack

import concourse.mybir as mybir
from concourse.masks import make_identity

F32 = mybir.dt.float32
BF16 = mybir.dt.bfloat16
U32 = mybir.dt.uint32
U8 = mybir.dt.uint8
I32 = mybir.dt.int32
FP8X4 = mybir.dt.float8_e4m3fn_x4
ALU = mybir.AluOpType
SIN = mybir.ActivationFunctionType.Sin

BATCH, SEQ, D_MODEL, HEADS, D_HEAD, D_LATENT, D_ROPE = 4, 1024, 1024, 4, 128, 512, 128
ROPE_BASE = 10000.0

P = 128
PACK = 4
K_PASS = P * PACK
H_PASSES = D_MODEL // K_PASS
SLOTS = SEQ // P
LINE = 256
PAIR = 2
GROUP = 4
PAIRS = BATCH * SLOTS // PAIR
GROUPS = BATCH * SLOTS // GROUP
ROPE_PAIRS = D_ROPE // 2
ROUND_MAGIC = 1.5 * 2.0**23

FLOPS = 2 * BATCH * SEQ * (D_MODEL * (D_LATENT + D_ROPE) + 2 * D_LATENT * HEADS * D_HEAD)


def tile_mla_pb_t_kernel(tc, h, w_ckv, w_k, w_kr, w_v, out_0, out_1):
    nc = tc.nc
    with ExitStack() as stack:
        stack.enter_context(tc.manual_schedule())
        consts = stack.enter_context(tc.tile_pool(name="consts", bufs=1))
        setup = stack.enter_context(tc.tile_pool(name="setup", bufs=1))
        h_pool = stack.enter_context(tc.tile_pool(name="h_pool", bufs=1))
        work = stack.enter_context(tc.tile_pool(name="work", bufs=2))
        out_pool = stack.enter_context(tc.tile_pool(name="out_pool", bufs=3))
        xt_psum = stack.enter_context(tc.psum_pool(name="xt_psum", bufs=2))
        c_psum = stack.enter_context(tc.psum_pool(name="c_psum", bufs=2))
        u_psum = stack.enter_context(tc.psum_pool(name="u_psum", bufs=1))
        kv_psum = stack.enter_context(tc.psum_pool(name="kv_psum", bufs=3))

        h_sb = h_pool.tile([P, BATCH, SLOTS * D_MODEL], BF16, align_bytes=LINE)
        h_rows = h.rearrange("b (p t) d -> p b (t d)", t=SLOTS)

        def load_h(batches, tiles):
            rows = slice(tiles.start * D_MODEL, tiles.stop * D_MODEL)
            nc.sync.dma_start(out=h_sb[:, batches, rows], in_=h_rows[:, batches, rows])

        wc_raw = setup.tile([P, H_PASSES, PACK, D_LATENT], BF16, align_bytes=LINE)
        wr_raw = setup.tile([P, H_PASSES, PACK, D_ROPE], BF16, align_bytes=LINE)
        wk_raw = setup.tile([P, PACK, HEADS * D_HEAD], BF16, align_bytes=LINE)
        wv_raw = setup.tile([P, PACK, HEADS * D_HEAD], BF16, align_bytes=LINE)
        for g in range(H_PASSES):
            nc.sync.dma_start(
                out=wc_raw[:, g].rearrange("p (u e) c -> p u (e c)", e=2),
                in_=w_ckv[g * K_PASS : (g + 1) * K_PASS, :].rearrange("(u p e) c -> p u (e c)", p=P, e=2),
            )
        load_h(slice(0, 1), slice(0, PAIR))
        nc.sync.dma_start(
            out=wr_raw[:].rearrange("p g (u e) c -> p (g u) (e c)", e=2),
            in_=w_kr.rearrange("(a p e) c -> p a (e c)", p=P, e=2),
        )
        load_h(slice(0, 1), slice(PAIR, GROUP))
        nc.sync.dma_start(
            out=wk_raw[:].rearrange("p j n -> p (j n)"),
            in_=w_k.rearrange("(p j) n -> p (j n)", j=PACK),
        )
        nc.sync.dma_start(
            out=wv_raw[:].rearrange("p j n -> p (j n)"),
            in_=w_v.rearrange("(p j) n -> p (j n)", j=PACK),
        )
        load_h(slice(0, 1), slice(GROUP, SLOTS))
        load_h(slice(1, 2), slice(0, SLOTS))
        load_h(slice(2, BATCH), slice(0, SLOTS))

        pos_i = setup.tile([P, SLOTS], I32, align_bytes=LINE)
        nc.gpsimd.iota(pos_i[:], pattern=[[1, SLOTS]], base=0, channel_multiplier=SLOTS)
        ident = consts.tile([P, P], F32, align_bytes=LINE)
        make_identity(nc, ident[:])

        turns = setup.tile([P, SLOTS, ROPE_PAIRS], F32, align_bytes=LINE)
        nc.vector.tensor_scalar_mul(out=turns[:, :, 0], in0=pos_i[:], scalar1=1.0 / (2.0 * math.pi))
        width = 1
        while width < ROPE_PAIRS:
            nc.vector.tensor_scalar_mul(
                out=turns[:, :, width : 2 * width],
                in0=turns[:, :, 0:width],
                scalar1=ROPE_BASE ** (-2.0 * width / D_ROPE),
            )
            width *= 2
        whole = setup.tile([P, SLOTS, ROPE_PAIRS], F32, align_bytes=LINE)
        nc.vector.tensor_scalar(
            out=whole[:],
            in0=turns[:],
            scalar1=ROUND_MAGIC,
            scalar2=ROUND_MAGIC,
            op0=ALU.add,
            op1=ALU.subtract,
        )
        frac = setup.tile([P, SLOTS, ROPE_PAIRS], F32, align_bytes=LINE)
        nc.vector.tensor_sub(out=frac[:], in0=turns[:], in1=whole[:])
        quarter = setup.tile([P, SLOTS, ROPE_PAIRS], F32, align_bytes=LINE)
        nc.vector.scalar_tensor_tensor(
            out=quarter[:], in0=frac[:], scalar=-1.0, in1=frac[:], op0=ALU.mult, op1=ALU.max
        )
        nc.vector.tensor_scalar(
            out=quarter[:], in0=quarter[:], scalar1=-1.0, scalar2=0.25, op0=ALU.mult, op1=ALU.add
        )
        cos_tab = consts.tile([P, SLOTS, ROPE_PAIRS], F32, align_bytes=LINE)
        sin_tab = consts.tile([P, SLOTS, ROPE_PAIRS, 2], F32, align_bytes=LINE)
        nc.scalar.activation(out=sin_tab[:, :, :, 0], in_=frac[:], func=SIN, scale=-2.0 * math.pi)
        nc.scalar.activation(out=cos_tab[:], in_=quarter[:], func=SIN, scale=2.0 * math.pi)

        hg_tiles, hq_tiles, cg_tiles, cq_tiles, prod_tiles, out_tiles = {}, {}, {}, {}, {}, {}

        def transpose_h(pair):
            b, slot = divmod(pair * PAIR, SLOTS)
            words = h_sb[:, b].bitcast(F32)
            hg = work.tile([P, PAIR * H_PASSES * P * PACK], BF16, align_bytes=LINE)
            hg_tiles[pair] = hg
            hg_words = hg[:].bitcast(F32).rearrange(
                "p (i g n u) -> p i g n u", i=PAIR, g=H_PASSES, u=2
            )
            for i in range(PAIR):
                first = (slot + i) * (D_MODEL // 2)
                xt = xt_psum.tile([P, 2 * H_PASSES, P], F32)
                for block in range(2 * H_PASSES):
                    nc.tensor.transpose(
                        xt[:, block, :], words[:, first + block * P : first + (block + 1) * P], ident[:]
                    )
                nc.scalar.copy(
                    out=hg_words[:, i], in_=xt[:].rearrange("p (g u) n -> p g n u", u=2)
                )

        def quantise_h(pair):
            hq = work.tile([P, PAIR, H_PASSES, P], U32, align_bytes=LINE)
            hs = work.tile([P, PAIR, H_PASSES, P], U8, align_bytes=LINE)
            hq_tiles[pair] = (hq, hs)
            nc.vector.quantize_mx(
                out=hq[:].rearrange("p i g n -> p (i g n)").bitcast(FP8X4),
                scales=hs[:].rearrange("p i g n -> p (i g n)"),
                in_=hg_tiles[pair][:],
            )

        def latent_tile(pair, i):
            hq, hs = hq_tiles[pair]
            if i == 0:
                cg = work.tile([P, PAIR, P, PACK], BF16, align_bytes=LINE)
                cg_tiles[pair] = cg
            c_ps = c_psum.tile([P, PACK, P], F32)
            for j in range(PACK):
                for g in range(H_PASSES):
                    nc.tensor.matmul_mx(
                        out=c_ps[:, j, :],
                        lhsT=wc_q[:, g, j, :].bitcast(FP8X4),
                        lhsT_scale=wc_s[:, g, j, :],
                        rhs=hq[:, i, g, :].bitcast(FP8X4),
                        rhs_scale=hs[:, i, g, :],
                        start=(g == 0),
                        stop=(g == H_PASSES - 1),
                    )
            nc.vector.tensor_copy(
                out=cg_tiles[pair][:, i], in_=c_ps[:].rearrange("p j n -> p n j")
            )

        def quantise_latent(pair):
            cg = cg_tiles[pair]
            cq = work.tile([P, PAIR, P], U32, align_bytes=LINE)
            cs = work.tile([P, PAIR, P], U8, align_bytes=LINE)
            cq_tiles[pair] = (cq, cs)
            nc.vector.quantize_mx(
                out=cq[:].rearrange("p i n -> p (i n)").bitcast(FP8X4),
                scales=cs[:].rearrange("p i n -> p (i n)"),
                in_=cg[:].rearrange("p i n j -> p (i n j)"),
            )

        def rotary_products(pair):
            hq, hs = hq_tiles[pair]
            u_ps = u_psum.tile([P, PAIR, ROPE_PAIRS, 2], F32)
            for i in range(PAIR):
                for g in range(H_PASSES):
                    nc.tensor.matmul_mx(
                        out=u_ps[:, i].rearrange("p r e -> p (r e)"),
                        lhsT=hq[:, i, g, :].bitcast(FP8X4),
                        lhsT_scale=hs[:, i, g, :],
                        rhs=wr_q[:, g, :].bitcast(FP8X4),
                        rhs_scale=wr_s[:, g, :],
                        start=(g == 0),
                        stop=(g == H_PASSES - 1),
                    )
            slot = (pair * PAIR) % SLOTS
            prod = work.tile([P, 2, PAIR, ROPE_PAIRS, 2], F32, align_bytes=LINE)
            prod_tiles[pair] = prod
            nc.vector.tensor_tensor(
                out=prod[:, 0],
                in0=u_ps[:],
                in1=cos_tab[:, slot : slot + PAIR, :].unsqueeze(3).to_broadcast([P, PAIR, ROPE_PAIRS, 2]),
                op=ALU.mult,
            )
            nc.vector.tensor_tensor(
                out=prod[:, 1],
                in0=u_ps[:, :, :, ::-1],
                in1=sin_tab[:, slot : slot + PAIR],
                op=ALU.mult,
            )

        def rotary_sum(pair):
            k_sb = out_tiles[pair // 2][0]
            prod = prod_tiles[pair]
            first = (pair % 2) * PAIR
            nc.vector.tensor_add(
                out=k_sb[:, 0, first : first + PAIR, D_HEAD:],
                in0=prod[:, 0].rearrange("p i r e -> p i (r e)"),
                in1=prod[:, 1].rearrange("p i r e -> p i (r e)"),
            )

        def rotary_copies(pair):
            k_sb = out_tiles[pair // 2][0]
            first = (pair % 2) * PAIR
            nc.vector.tensor_copy(
                out=k_sb[:, 1:, first : first + PAIR, D_HEAD:],
                in_=k_sb[:, 0:1, first : first + PAIR, D_HEAD:].to_broadcast(
                    [P, HEADS - 1, PAIR, D_ROPE]
                ),
            )

        def keys_values_tile(pair, i):
            cq, cs = cq_tiles[pair]
            k_sb, v_sb = out_tiles[pair // 2]
            slot = (pair % 2) * PAIR + i
            v_copy = nc.vector.tensor_copy if pair == PAIRS - 1 else nc.scalar.copy
            for codes, scales, dst, copy in (
                (wk_q, wk_s, k_sb[:, :, slot, 0:D_HEAD], nc.scalar.copy),
                (wv_q, wv_s, v_sb[:, :, slot, :], v_copy),
            ):
                kv_ps = kv_psum.tile([P, HEADS, D_HEAD], F32)
                nc.tensor.matmul_mx(
                    out=kv_ps[:].rearrange("p n d -> p (n d)"),
                    lhsT=cq[:, i, :].bitcast(FP8X4),
                    lhsT_scale=cs[:, i, :],
                    rhs=codes[:].bitcast(FP8X4),
                    rhs_scale=scales[:],
                    start=True,
                    stop=True,
                )
                copy(out=dst, in_=kv_ps[:])

        def store(dram, sbuf, group, first, count):
            b, slot = divmod(group * GROUP + first, SLOTS)
            nc.sync.dma_start(
                out=dram[b].rearrange("n (p t) d -> p n t d", t=SLOTS)[:, :, slot : slot + count, :],
                in_=sbuf[:, :, first : first + count, :],
            )

        def store_pair(pair):
            group, odd = divmod(pair, 2)
            k_sb, v_sb = out_tiles[group]
            store(out_0, k_sb, group, odd * PAIR, PAIR)
            if group in (0, GROUPS - 1):
                store(out_1, v_sb, group, odd * PAIR, PAIR)
            elif odd:
                store(out_1, v_sb, group, 0, GROUP)

        def store_last_tile(i):
            for dram, sbuf in zip((out_0, out_1), out_tiles[GROUPS - 1]):
                store(dram, sbuf, GROUPS - 1, GROUP - PAIR + i, 1)

        def quantise(grouped, codes, scales):
            nc.vector.quantize_mx(out=codes.bitcast(FP8X4), scales=scales, in_=grouped)

        wc_q = consts.tile([P, H_PASSES, PACK, P], U32, align_bytes=LINE)
        wc_s = consts.tile([P, H_PASSES, PACK, P], U8, align_bytes=LINE)
        wc_g = setup.tile([P, H_PASSES, PACK, P, PACK], BF16, align_bytes=LINE)
        for g in range(H_PASSES):
            nc.vector.tensor_copy(
                out=wc_g[:, g], in_=wc_raw[:, g].rearrange("p t (m j) -> p j m t", j=PACK)
            )
        transpose_h(0)
        nc.scalar.activation(out=sin_tab[:, :, :, 1], in_=frac[:], func=SIN, scale=2.0 * math.pi)
        for g in range(H_PASSES):
            quantise(
                wc_g[:, g].rearrange("p j m t -> p (j m t)"),
                wc_q[:, g].rearrange("p j m -> p (j m)"),
                wc_s[:, g].rearrange("p j m -> p (j m)"),
            )
        quantise_h(0)

        wr_q = consts.tile([P, H_PASSES, D_ROPE], U32, align_bytes=LINE)
        wr_s = consts.tile([P, H_PASSES, D_ROPE], U8, align_bytes=LINE)
        wr_g = setup.tile([P, H_PASSES, D_ROPE, PACK], BF16, align_bytes=LINE)
        nc.vector.tensor_copy(out=wr_g[:], in_=wr_raw[:].rearrange("p g t c -> p g c t"))
        transpose_h(1)
        quantise(
            wr_g[:].rearrange("p g c t -> p (g c t)"),
            wr_q[:].rearrange("p g c -> p (g c)"),
            wr_s[:].rearrange("p g c -> p (g c)"),
        )

        wk_q = consts.tile([P, HEADS * D_HEAD], U32, align_bytes=LINE)
        wk_s = consts.tile([P, HEADS * D_HEAD], U8, align_bytes=LINE)
        wv_q = consts.tile([P, HEADS * D_HEAD], U32, align_bytes=LINE)
        wv_s = consts.tile([P, HEADS * D_HEAD], U8, align_bytes=LINE)
        wk_g = setup.tile([P, HEADS * D_HEAD, PACK], BF16, align_bytes=LINE)
        wv_g = setup.tile([P, HEADS * D_HEAD, PACK], BF16, align_bytes=LINE)
        nc.scalar.copy(out=wk_g[:], in_=wk_raw[:].rearrange("p j n -> p n j"))
        nc.scalar.copy(out=wv_g[:], in_=wv_raw[:].rearrange("p j n -> p n j"))

        for step in range(PAIRS + 1):
            entering = step < PAIRS
            leaving = step >= 1
            if entering and step % 2 == 0:
                k_sb = out_pool.tile([P, HEADS, GROUP, D_HEAD + D_ROPE], F32, align_bytes=LINE)
                v_sb = out_pool.tile([P, HEADS, GROUP, D_HEAD], F32, align_bytes=LINE)
                out_tiles[step // 2] = (k_sb, v_sb)
            if entering:
                latent_tile(step, 0)
                rotary_products(step)
            if leaving:
                keys_values_tile(step - 1, 0)
                if step == PAIRS:
                    store_last_tile(0)
            if step + 1 < PAIRS:
                quantise_h(step + 1)
            if entering:
                latent_tile(step, 1)
                rotary_sum(step)
            if leaving:
                keys_values_tile(step - 1, 1)
                if step == PAIRS:
                    store_last_tile(1)
            if entering:
                quantise_latent(step)
                rotary_copies(step)
            if step == 0:
                quantise(wk_g[:].rearrange("p n j -> p (n j)"), wk_q[:], wk_s[:])
                quantise(wv_g[:].rearrange("p n j -> p (n j)"), wv_q[:], wv_s[:])
            if leaving and step < PAIRS:
                store_pair(step - 1)
            if step + 2 < PAIRS:
                transpose_h(step + 2)
